import numpy as np
import ml_dtypes


def mxq(x, axis, fmt="e4m3"):
    dtype, down = {"e4m3": (ml_dtypes.float8_e4m3fn, 7), "e5m2": (ml_dtypes.float8_e5m2, 14)}[fmt]
    v = np.moveaxis(np.asarray(x, np.float32).astype(ml_dtypes.bfloat16).astype(np.float64), axis, -1)
    blocks = v.reshape(v.shape[:-1] + (-1, 32))
    amax = np.abs(blocks).max(-1, keepdims=True)
    byte = np.maximum(np.where(amax > 0, np.frexp(amax)[1] - 1 + 127, 0) - down, 1)
    scale = np.exp2(byte - 127.0)
    codes = (blocks / scale).astype(np.float32).astype(dtype).astype(np.float64)
    return np.moveaxis((codes * scale).reshape(v.shape), -1, axis)


WIDE = False


def mx_kscale(k):
    if not WIDE:
        return np.ones(k)
    levels = np.array([10, -10, 5, -5, 0])
    a = np.random.permutation(np.resize(levels, k // 512 * 4)).reshape(k // 512, 4)
    idx = np.arange(k)
    return np.exp2(a[idx // 512, idx % 128 // 32])


BF16 = ml_dtypes.bfloat16


def bf(x):
    return np.asarray(x, np.float32).astype(BF16)


def f64(x):
    return np.asarray(x).astype(np.float64)


B, T, C = 8, 512, 512
EPS = 1e-8


def sigmoid(z):
    return 1.0 / (1.0 + np.exp(-z))


def setup_inputs():
    s = mx_kscale(C)
    t = mx_kscale(C)
    g = 1.0 / np.sqrt(C)
    return {
        "x": bf(np.random.standard_normal((B, T, C)) * s),
        "a0": bf(np.random.standard_normal((B, C)) * t),
        "b0": bf(0.5 + np.random.uniform(size=(B, C))),
        "x_prev0": bf(np.random.standard_normal((B, C)) * s),
        "w": bf((0.5 + 2.0 * np.random.uniform(size=C)) / T),
        "u": bf(np.random.standard_normal(C) * 0.5),
        "mu_r": bf(np.random.uniform(size=C)),
        "mu_k": bf(np.random.uniform(size=C)),
        "mu_v": bf(np.random.uniform(size=C)),
        "W_r": bf(np.random.standard_normal((C, C)) * g / s[None, :]),
        "W_k": bf(np.random.standard_normal((C, C)) * g / s[None, :]),
        "W_v": bf(np.random.standard_normal((C, C)) * g / s[None, :] * t[:, None]),
        "W_out": bf(np.random.standard_normal((C, C)) * 2.0 * g / t[None, :]),
    }


def reference(x, a0, b0, x_prev0, w, u, mu_r, mu_k, mu_v, W_r, W_k, W_v, W_out):
    x, a0, b0, x_prev0 = f64(x), f64(a0), f64(b0), f64(x_prev0)
    w, u = f64(w), f64(u)
    mu_r, mu_k, mu_v = f64(mu_r), f64(mu_k), f64(mu_v)
    x_shift = np.concatenate([x_prev0[:, None, :], x[:, :-1, :]], axis=1)
    xr = mu_r * x + (1.0 - mu_r) * x_shift
    xk = mu_k * x + (1.0 - mu_k) * x_shift
    xv = mu_v * x + (1.0 - mu_v) * x_shift
    r = sigmoid(mxq(xr, 2, "e4m3") @ mxq(f64(W_r), 1, "e4m3").T)
    k = mxq(xk, 2, "e4m3") @ mxq(f64(W_k), 1, "e4m3").T
    v = mxq(xv, 2, "e4m3") @ mxq(f64(W_v), 1, "e4m3").T
    ek = np.exp(u + k)
    steps = np.arange(1, T + 1).astype(np.float64)
    decay_pow = np.exp(-w[None, :] * steps[:, None])
    a_t = a0[:, None, :] * decay_pow[None]
    b_t = b0[:, None, :] * decay_pow[None]
    wkv = (a_t + ek * v) / (b_t + ek + EPS)
    h = r * wkv
    return mxq(h, 2, "e4m3") @ mxq(f64(W_out), 1, "e4m3").T

@@ -1,0 +1,409 @@
+from contextlib import ExitStack
+
+import concourse.bass as bass
+import concourse.masks as masks
+import concourse.mybir as mybir
+import concourse.tile as tile
+
+FP8X4 = mybir.dt.float8_e4m3fn_x4
+BF16 = mybir.dt.bfloat16
+F32 = mybir.dt.float32
+I32 = mybir.dt.int32
+U32 = mybir.dt.uint32
+U8 = mybir.dt.uint8
+ALU = mybir.AluOpType
+AF = mybir.ActivationFunctionType
+
+P = 128
+B = 8
+T = 512
+C = 512
+J = 4
+EPS = 1e-8
+PADC = 16
+FLOPS = 4 * 2 * B * T * C * C
+MANUAL = False
+
+
+def tile_rwkv_timemix_pa_t_kernel(
+    tc, x, a0, b0, x_prev0, w, u, mu_r, mu_k, mu_v, W_r, W_k, W_v, W_out, out
+):
+    nc = tc.nc
+    with ExitStack() as ctx:
+        if MANUAL:
+            ctx.enter_context(tc.manual_schedule())
+        const = ctx.enter_context(tc.tile_pool(name="const", bufs=1))
+        work = ctx.enter_context(tc.tile_pool(name="work", bufs=2))
+        psum = ctx.enter_context(tc.psum_pool(name="psum", bufs=1))
+
+        prm = const.tile([P, C], BF16)
+        nc.vector.memset(prm[:], 0.0)
+        for r, vec in enumerate((w, u, mu_r, mu_k, mu_v)):
+            nc.scalar.dma_start(out=prm[r : r + 1, :], in_=vec.rearrange("(o c) -> o c", o=1))
+        nc.scalar.dma_start(out=prm[8:16, :], in_=a0)
+        nc.scalar.dma_start(out=prm[16:24, :], in_=b0)
+        nc.scalar.dma_start(out=prm[24:32, :], in_=x_prev0)
+        nc.sync.dma_start(
+            out=prm[32:64, :], in_=x.rearrange("b (i t) c -> (b i) t c", t=P)[:, P - 1, :]
+        )
+
+        xn = {}
+
+        def load_x(b):
+            xn[b] = work.tile([P, 4, C], BF16, name="xn", tag="xn", bufs=3)
+            nc.sync.dma_start(out=xn[b][:], in_=x[b].rearrange("(i p) c -> p i c", p=P))
+
+        wnat = {}
+
+        def load_w(key, wap):
+            wnat[key] = const.tile([P, 4, C], BF16, name="wn" + key, tag="wn" + key)
+            nc.sync.dma_start(out=wnat[key][:], in_=wap.rearrange("(a p) c -> p a c", p=P))
+
+        load_x(0)
+        load_w("k", W_k)
+        load_w("r", W_r)
+        load_w("v", W_v)
+        load_x(1)
+        load_w("o", W_out)
+
+        ident = const.tile([P, P], BF16)
+        masks.make_identity(nc, ident[:])
+        it_i = const.tile([P, T], I32)
+        nc.gpsimd.iota(it_i[:], pattern=[[1, T]], base=1, channel_multiplier=0)
+        dmat = const.tile([P, P], BF16)
+        nc.vector.tensor_copy(out=dmat[:, 0:1], in_=ident[:, 0:1])
+        nc.vector.tensor_tensor(
+            out=dmat[:, 1:P], in0=ident[:, 1:P], in1=ident[:, 0 : P - 1], op=ALU.subtract
+        )
+        sel = const.tile([P, B, 4, 8], BF16)
+        nc.vector.memset(sel[:], 0.0)
+        nc.vector.tensor_scalar(
+            out=sel[:, :, 0, 0], in0=ident[:, 24:32], scalar1=-1.0, scalar2=None, op0=ALU.mult
+        )
+        nc.vector.tensor_scalar(
+            out=sel[:, :, 1:4, 0],
+            in0=ident[:, 32:64].rearrange("p (b i) -> p b i", i=4)[:, :, 0:3],
+            scalar1=-1.0,
+            scalar2=None,
+            op0=ALU.mult,
+        )
+        it_f = const.tile([P, T], F32)
+        nc.vector.tensor_copy(out=it_f[:], in_=it_i[:])
+
+        pt = psum.tile([P, J, P], BF16, name="pt", tag="aux", bufs=3)
+        for j in range(J):
+            nc.tensor.transpose(out=pt[:, j, :], in_=prm[:, j * P : (j + 1) * P], identity=ident[:])
+        pf = const.tile([P, J, 32], F32)
+        nc.vector.tensor_copy(out=pf[:], in_=pt[:, :, 0:32])
+        xpT = const.tile([P, J, B], BF16)
+        nc.vector.tensor_copy(out=xpT[:], in_=pt[:, :, 24:32])
+        negw = const.tile([P, J], F32)
+        nc.vector.tensor_scalar(out=negw[:], in0=pf[:, :, 0], scalar1=-1.0, scalar2=None, op0=ALU.mult)
+        lnb = const.tile([P, J, B], F32)
+        nc.scalar.activation(out=lnb[:], in_=pf[:, :, 16:24], func=AF.Ln)
+        rb0 = const.tile([P, J, B], F32)
+        nc.vector.reciprocal(out=rb0[:], in_=pf[:, :, 16:24])
+        g0 = const.tile([P, J, B], F32)
+        nc.vector.tensor_tensor(out=g0[:], in0=pf[:, :, 8:16], in1=rb0[:], op=ALU.mult)
+        et = const.tile([P, J, B], F32)
+        nc.vector.tensor_scalar(out=et[:], in0=rb0[:], scalar1=EPS, scalar2=None, op0=ALU.mult)
+        g0e = const.tile([P, J, B], F32)
+        nc.vector.tensor_tensor(out=g0e[:], in0=g0[:], in1=et[:], op=ALU.mult)
+        g0h = const.tile([P, J, B], F32)
+        nc.vector.tensor_scalar(out=g0h[:], in0=g0[:], scalar1=0.5, scalar2=None, op0=ALU.mult)
+        beta = const.tile([P, J, B], F32)
+        nc.vector.tensor_tensor(
+            out=beta[:], in0=pf[:, :, 1:2].to_broadcast([P, J, B]), in1=lnb[:], op=ALU.subtract
+        )
+        dtab = const.tile([P, J, T], F32)
+        for j in range(J):
+            nc.scalar.activation(
+                out=dtab[:, j, :], in_=it_f[:], func=AF.Exp, scale=negw[:, j : j + 1]
+            )
+
+        xT = {}
+        dd = {}
+
+        def make_dd(b, j):
+            t = psum.tile([P, T], F32, name="dd", tag="dd", bufs=2)
+            dd[(b, j)] = t
+            for i in range(4):
+                nc.tensor.matmul(
+                    out=t[:, i * P : (i + 1) * P],
+                    lhsT=xn[b][:, i, j * P : (j + 1) * P],
+                    rhs=dmat[:],
+                    start=(i == 0),
+                    stop=False,
+                )
+            nc.tensor.matmul(
+                out=t[:].rearrange("p (i e) -> p i e", e=P)[:, :, 0:8],
+                lhsT=prm[:, j * P : (j + 1) * P],
+                rhs=sel[:, b, :, :],
+                start=False,
+                stop=True,
+            )
+
+        xtp = {}
+
+        def transposes(b, jh):
+            xt = psum.tile([P, 2, T], BF16, name="xt", tag="aux", bufs=3)
+            xtp[(b, jh)] = xt
+            for jj in range(2):
+                j = 2 * jh + jj
+                for i in range(4):
+                    nc.tensor.transpose(
+                        out=xt[:, jj, i * P : (i + 1) * P],
+                        in_=xn[b][:, i, j * P : (j + 1) * P],
+                        identity=ident[:],
+                    )
+
+        def evac_xT(b):
+            xT[b] = work.tile([P, J, PADC + T], BF16, name="xT", tag="xT", bufs=2)
+            nc.gpsimd.tensor_copy(out=xT[b][:, :, PADC - 1 : PADC], in_=xpT[:, :, b : b + 1])
+            for jh in range(2):
+                nc.scalar.copy(out=xT[b][:, 2 * jh : 2 * jh + 2, PADC:], in_=xtp[(b, jh)][:])
+
+        wc = {}
+        ws = {}
+        wg = {}
+
+        def prep_w(key):
+            wg[key] = const.tile([P, C, J], BF16, name="wg", tag="wg", bufs=2, align_bytes=64)
+            for h in range(2):
+                wt = psum.tile([P, 2, J, P], BF16, name="wt", tag="aux", bufs=3)
+                for a in range(2):
+                    for j in range(J):
+                        nc.tensor.transpose(
+                            out=wt[:, a, j, :],
+                            in_=wnat[key][:, 2 * h + a, j * P : (j + 1) * P],
+                            identity=ident[:],
+                        )
+                nc.scalar.copy(
+                    out=wg[key][:, 256 * h : 256 * h + 256, :].rearrange("p (a o) j -> p a o j", a=2),
+                    in_=wt[:].rearrange("p a j o -> p a o j"),
+                )
+
+        def quant_w(key):
+            wc[key] = const.tile([P, C], U32, name="wc" + key, tag="wc" + key, align_bytes=64)
+            ws[key] = const.tile([P, C], U8, name="ws" + key, tag="ws" + key, align_bytes=64)
+            nc.vector.quantize_mx(
+                out=wc[key][:].bitcast(FP8X4),
+                scales=ws[key][:],
+                in_=wg[key][:].rearrange("p o j -> p (o j)"),
+            )
+
+        pl = {}
+        gr = {}
+        xc = {}
+        xs = {}
+        MS = ("r", "k", "v")
+
+        def mix(b, j, mi):
+            m = MS[mi]
+            if j == 0:
+                pl[m] = work.tile([P, J, T], BF16, name="pl" + m, tag="pl" + m, bufs=1)
+            nc.vector.scalar_tensor_tensor(
+                out=pl[m][:, j, :],
+                in0=dd[(b, j)][:],
+                scalar=pf[:, j, 2 + mi : 3 + mi],
+                in1=xT[b][:, j, PADC - 1 : PADC - 1 + T],
+                op0=ALU.mult,
+                op1=ALU.add,
+            )
+
+        def regroup(b, m):
+            gr[m] = work.tile([P, T, J], BF16, name="gr", tag="gr", bufs=3, align_bytes=64)
+            nc.vector.tensor_copy(
+                out=gr[m][:].rearrange("p (c i) t -> p c t i", i=4),
+                in_=pl[m][:].rearrange("p t (c i) -> p c t i", i=4),
+            )
+
+        def quant_x(b, m):
+            xc[(b, m)] = work.tile([P, T], U32, name="xc" + m, tag="xc" + m, bufs=2, align_bytes=64)
+            xs[(b, m)] = work.tile([P, T], U8, name="xs" + m, tag="xs" + m, bufs=2, align_bytes=64)
+            nc.vector.quantize_mx(
+                out=xc[(b, m)][:].bitcast(FP8X4),
+                scales=xs[(b, m)][:],
+                in_=gr[m][:].rearrange("p w t -> p (w t)"),
+            )
+
+        ee = {}
+        th = {}
+        qq = {}
+        dn = {}
+
+        def stage1(b, j):
+            if j == 0:
+                ee[b] = work.tile([P, J, T], F32, name="ee", tag="ee", bufs=2)
+                th[b] = work.tile([P, J, T], F32, name="th", tag="th", bufs=2)
+                qq[b] = work.tile([P, J, T], F32, name="qq", tag="qq", bufs=2)
+                dn[b] = work.tile([P, J, T], F32, name="dn", tag="dn", bufs=2)
+            ps = {}
+            for m in ("k", "r", "v"):
+                ps[m] = psum.tile([P, T], F32, name="s1" + m, tag="s1", bufs=3)
+                nc.tensor.matmul_mx(
+                    out=ps[m][:],
+                    lhsT=wc[m][:, j * P : (j + 1) * P].bitcast(FP8X4),
+                    lhsT_scale=ws[m][:, j * P : (j + 1) * P],
+                    rhs=xc[(b, m)][:].bitcast(FP8X4),
+                    rhs_scale=xs[(b, m)][:],
+                    start=True,
+                    stop=True,
+                )
+            nc.scalar.activation(
+                out=ee[b][:, j, :], in_=ps["k"][:], func=AF.Exp, bias=beta[:, j, b : b + 1]
+            )
+            nc.scalar.activation(out=th[b][:, j, :], in_=ps["r"][:], func=AF.Tanh, scale=0.5)
+            nc.gpsimd.tensor_tensor(
+                out=dn[b][:, j, :], in0=ee[b][:, j, :], in1=dtab[:, j, :], op=ALU.add
+            )
+            nc.vector.scalar_tensor_tensor(
+                out=qq[b][:, j, :],
+                in0=ps["v"][:],
+                scalar=g0[:, j, b : b + 1],
+                in1=ee[b][:, j, :],
+                op0=ALU.subtract,
+                op1=ALU.mult,
+            )
+
+        def recip(b):
+            for j in range(J):
+                nc.scalar.activation(
+                    out=dn[b][:, j, :], in_=dn[b][:, j, :], func=AF.Ln, bias=et[:, j, b : b + 1]
+                )
+            nc.scalar.activation(out=dn[b][:], in_=dn[b][:], func=AF.Exp, scale=-1.0)
+
+        def wkv_x(b, j):
+            nc.vector.scalar_tensor_tensor(
+                out=qq[b][:, j, :],
+                in0=qq[b][:, j, :],
+                scalar=g0e[:, j, b : b + 1],
+                in1=dn[b][:, j, :],
+                op0=ALU.subtract,
+                op1=ALU.mult,
+            )
+
+        def wkv_y(b, j):
+            nc.scalar.activation(
+                out=qq[b][:, j, :],
+                in_=qq[b][:, j, :],
+                func=AF.Identity,
+                scale=0.5,
+                bias=g0h[:, j, b : b + 1],
+            )
+
+        hg = {}
+        hc = {}
+        hs = {}
+
+        def gate(b):
+            hg[b] = work.tile([P, T, J], BF16, name="hg", tag="hg", bufs=2, align_bytes=64)
+            nc.vector.scalar_tensor_tensor(
+                out=hg[b][:],
+                in0=th[b][:].rearrange("p j t -> p t j"),
+                scalar=1.0,
+                in1=qq[b][:].rearrange("p j t -> p t j"),
+                op0=ALU.add,
+                op1=ALU.mult,
+            )
+
+        def quant_h(b):
+            hc[b] = work.tile([P, T], U32, name="hc", tag="hc", bufs=2, align_bytes=64)
+            hs[b] = work.tile([P, T], U8, name="hs", tag="hs", bufs=2, align_bytes=64)
+            nc.vector.quantize_mx(
+                out=hc[b][:].bitcast(FP8X4),
+                scales=hs[b][:],
+                in_=hg[b][:].rearrange("p w t -> p (w t)"),
+            )
+
+        def stage2(b):
+            ost = work.tile([P, 4, C], F32, name="ost", tag="ost", bufs=2)
+            for i in range(4):
+                po = psum.tile([P, C], F32, name="po", tag="aux", bufs=3)
+                nc.tensor.matmul_mx(
+                    out=po[:],
+                    lhsT=hc[b][:, i * P : (i + 1) * P].bitcast(FP8X4),
+                    lhsT_scale=hs[b][:, i * P : (i + 1) * P],
+                    rhs=wc["o"][:].bitcast(FP8X4),
+                    rhs_scale=ws["o"][:],
+                    start=True,
+                    stop=True,
+                )
+                nc.scalar.copy(out=ost[:, i, :], in_=po[:])
+            nc.sync.dma_start(out=out[b].rearrange("(i p) c -> p i c", p=P), in_=ost[:])
+
+        transposes(0, 0)
+        transposes(0, 1)
+        evac_xT(0)
+        make_dd(0, 0)
+        make_dd(0, 1)
+        for key in ("k", "r", "v"):
+            prep_w(key)
+            if key == "r":
+                quant_w("k")
+        for it in range(B + 2):
+            a = it
+            bb = it - 1
+            c = it - 2
+            has_a = a < B
+            has_n = a + 1 < B
+            has_b = 0 <= bb < B
+            has_c = c >= 0
+            stts = [(j, mi) for j in range(J) for mi in (1, 0, 2)] if has_a else []
+            done = [0]
+
+            def emit_stt(n):
+                for q in range(n):
+                    if done[0] < len(stts):
+                        j, mi = stts[done[0]]
+                        mix(a, j, mi)
+                        done[0] += 1
+                        if done[0] == 3:
+                            make_dd(a, 2)
+                        if done[0] == 6:
+                            make_dd(a, 3)
+                        if done[0] == 9 and has_n:
+                            make_dd(a + 1, 0)
+                        if done[0] == 12 and has_n:
+                            make_dd(a + 1, 1)
+
+            if a + 2 < B:
+                load_x(a + 2)
+            for j in range(J):
+                if has_b:
+                    stage1(bb, j)
+                if has_n and j < 2:
+                    transposes(a + 1, j)
+                emit_stt(1)
+            if has_n:
+                evac_xT(a + 1)
+            if has_c:
+                for j in range(J):
+                    wkv_x(c, j)
+                for j in range(J):
+                    wkv_y(c, j)
+            emit_stt(3)
+            if it == 1:
+                prep_w("o")
+            if has_c:
+                gate(c)
+            emit_stt(2)
+            if it == 0:
+                quant_w("r")
+                quant_w("v")
+            if it == 1:
+                quant_w("o")
+            if has_c:
+                quant_h(c)
+            emit_stt(3)
+            if has_b:
+                recip(bb)
+            if has_c:
+                stage2(c)
+            if has_a:
+                regroup(a, "k")
+                regroup(a, "r")
+                quant_x(a, "k")
+                regroup(a, "v")
+                quant_x(a, "r")
+                quant_x(a, "v")

@@ -23,6 +23,9 @@ EPS = 1e-8
 PADC = 16
 FLOPS = 4 * 2 * B * T * C * C
 MANUAL = False
+Y_ENG = "act"
+G_ENG = {"k": "dve", "r": "dve", "v": "dve"}
+TAIL = False
 
 
 def tile_rwkv_timemix_pa_t_kernel(
@@ -87,6 +90,8 @@ def tile_rwkv_timemix_pa_t_kernel(
             scalar2=None,
             op0=ALU.mult,
         )
+        half = const.tile([P, 1], F32)
+        nc.vector.memset(half[:], 0.5)
         it_f = const.tile([P, T], F32)
         nc.vector.tensor_copy(out=it_f[:], in_=it_i[:])
 
@@ -213,10 +218,16 @@ def tile_rwkv_timemix_pa_t_kernel(
 
         def regroup(b, m):
             gr[m] = work.tile([P, T, J], BF16, name="gr", tag="gr", bufs=3, align_bytes=64)
-            nc.vector.tensor_copy(
-                out=gr[m][:].rearrange("p (c i) t -> p c t i", i=4),
-                in_=pl[m][:].rearrange("p t (c i) -> p c t i", i=4),
-            )
+            dst = gr[m][:].rearrange("p (c i) t -> p c t i", i=4)
+            src = pl[m][:].rearrange("p t (c i) -> p c t i", i=4)
+            if G_ENG[m] == "dve":
+                nc.vector.tensor_copy(out=dst, in_=src)
+            elif G_ENG[m] == "act":
+                nc.scalar.copy(out=dst, in_=src)
+            else:
+                nc.gpsimd.tensor_scalar(
+                    out=dst, in0=src, scalar1=1.0, scalar2=0.0, op0=ALU.mult, op1=ALU.add
+                )
 
         def quant_x(b, m):
             xc[(b, m)] = work.tile([P, T], U32, name="xc" + m, tag="xc" + m, bufs=2, align_bytes=64)
@@ -254,6 +265,14 @@ def tile_rwkv_timemix_pa_t_kernel(
                 out=ee[b][:, j, :], in_=ps["k"][:], func=AF.Exp, bias=beta[:, j, b : b + 1]
             )
             nc.scalar.activation(out=th[b][:, j, :], in_=ps["r"][:], func=AF.Tanh, scale=0.5)
+            nc.gpsimd.tensor_scalar(
+                out=th[b][:, j, :],
+                in0=th[b][:, j, :],
+                scalar1=1.0,
+                scalar2=1.0,
+                op0=ALU.mult,
+                op1=ALU.add,
+            )
             nc.gpsimd.tensor_tensor(
                 out=dn[b][:, j, :], in0=ee[b][:, j, :], in1=dtab[:, j, :], op=ALU.add
             )
@@ -284,13 +303,24 @@ def tile_rwkv_timemix_pa_t_kernel(
             )
 
         def wkv_y(b, j):
-            nc.scalar.activation(
-                out=qq[b][:, j, :],
-                in_=qq[b][:, j, :],
-                func=AF.Identity,
-                scale=0.5,
-                bias=g0h[:, j, b : b + 1],
-            )
+            if Y_ENG == "act":
+                nc.scalar.activation(
+                    out=qq[b][:, j, :],
+                    in_=qq[b][:, j, :],
+                    func=AF.Identity,
+                    scale=0.5,
+                    bias=g0h[:, j, b : b + 1],
+                )
+            else:
+                eng = nc.gpsimd if Y_ENG == "pool" else nc.vector
+                eng.tensor_scalar(
+                    out=qq[b][:, j, :],
+                    in0=qq[b][:, j, :],
+                    scalar1=half[:, 0:1],
+                    scalar2=g0h[:, j, b : b + 1],
+                    op0=ALU.mult,
+                    op1=ALU.add,
+                )
 
         hg = {}
         hc = {}
@@ -298,13 +328,11 @@ def tile_rwkv_timemix_pa_t_kernel(
 
         def gate(b):
             hg[b] = work.tile([P, T, J], BF16, name="hg", tag="hg", bufs=2, align_bytes=64)
-            nc.vector.scalar_tensor_tensor(
-                out=hg[b][:],
-                in0=th[b][:].rearrange("p j t -> p t j"),
-                scalar=1.0,
-                in1=qq[b][:].rearrange("p j t -> p t j"),
-                op0=ALU.add,
-                op1=ALU.mult,
+            nc.vector.tensor_tensor(
+                out=hg[b][:].rearrange("p (c i) j -> p c j i", i=4),
+                in0=th[b][:].rearrange("p j (c i) -> p c j i", i=4),
+                in1=qq[b][:].rearrange("p j (c i) -> p c j i", i=4),
+                op=ALU.mult,
             )
 
         def quant_h(b):

@@ -23,7 +23,7 @@ EPS = 1e-8
 PADC = 16
 FLOPS = 4 * 2 * B * T * C * C
 MANUAL = False
-Y_ENG = "act"
+Y_ENG = "pool"
 G_ENG = {"k": "dve", "r": "dve", "v": "dve"}
 TAIL = False
 

@@ -1,9 +1,7 @@
 from contextlib import ExitStack
 
-import concourse.bass as bass
 import concourse.masks as masks
 import concourse.mybir as mybir
-import concourse.tile as tile
 
 FP8X4 = mybir.dt.float8_e4m3fn_x4
 BF16 = mybir.dt.bfloat16
@@ -22,10 +20,9 @@ J = 4
 EPS = 1e-8
 PADC = 16
 FLOPS = 4 * 2 * B * T * C * C
-MANUAL = False
-Y_ENG = "pool"
-G_ENG = {"k": "dve", "r": "dve", "v": "dve"}
-TAIL = False
+MANUAL = True
+QPOS = (4, 6, 8, 10)
+NH = 2
 
 
 def tile_rwkv_timemix_pa_t_kernel(
@@ -37,18 +34,25 @@ def tile_rwkv_timemix_pa_t_kernel(
             ctx.enter_context(tc.manual_schedule())
         const = ctx.enter_context(tc.tile_pool(name="const", bufs=1))
         work = ctx.enter_context(tc.tile_pool(name="work", bufs=2))
-        psum = ctx.enter_context(tc.psum_pool(name="psum", bufs=1))
+        psum = ctx.enter_context(tc.psum_pool(name="psum", bufs=8))
 
-        prm = const.tile([P, C], BF16)
-        nc.vector.memset(prm[:], 0.0)
-        for r, vec in enumerate((w, u, mu_r, mu_k, mu_v)):
-            nc.scalar.dma_start(out=prm[r : r + 1, :], in_=vec.rearrange("(o c) -> o c", o=1))
-        nc.scalar.dma_start(out=prm[8:16, :], in_=a0)
-        nc.scalar.dma_start(out=prm[16:24, :], in_=b0)
-        nc.scalar.dma_start(out=prm[24:32, :], in_=x_prev0)
+        def bank(shape, dtype, name):
+            return psum.tile(shape, dtype, name=name, tag="ps", bufs=8)
+
+        prma = const.tile([P, C], BF16)
+        prmb = const.tile([P, C], BF16)
+        nc.vector.memset(prma[:], 0.0)
+        nc.vector.memset(prmb[:], 0.0)
         nc.sync.dma_start(
-            out=prm[32:64, :], in_=x.rearrange("b (i t) c -> (b i) t c", t=P)[:, P - 1, :]
+            out=prma[32:64, :], in_=x.rearrange("b (i t) c -> (b i) t c", t=P)[:, P - 1, :]
         )
+        for r, vec in enumerate((mu_r, mu_k, mu_v)):
+            nc.scalar.dma_start(out=prma[r : r + 1, :], in_=vec.rearrange("(o c) -> o c", o=1))
+        nc.scalar.dma_start(out=prma[24:32, :], in_=x_prev0)
+        for r, vec in enumerate((w, u)):
+            nc.scalar.dma_start(out=prmb[r : r + 1, :], in_=vec.rearrange("(o c) -> o c", o=1))
+        nc.scalar.dma_start(out=prmb[8:16, :], in_=a0)
+        nc.scalar.dma_start(out=prmb[16:24, :], in_=b0)
 
         xn = {}
 
@@ -68,11 +72,16 @@ def tile_rwkv_timemix_pa_t_kernel(
         load_w("v", W_v)
         load_x(1)
         load_w("o", W_out)
+        load_x(2)
 
         ident = const.tile([P, P], BF16)
         masks.make_identity(nc, ident[:])
         it_i = const.tile([P, T], I32)
         nc.gpsimd.iota(it_i[:], pattern=[[1, T]], base=1, channel_multiplier=0)
+        half = const.tile([P, 1], F32)
+        nc.vector.memset(half[:], 0.5)
+        dummy = const.tile([P, 1], F32)
+        nc.scalar.activation(out=dummy[:], in_=half[:], func=AF.Ln)
         dmat = const.tile([P, P], BF16)
         nc.vector.tensor_copy(out=dmat[:, 0:1], in_=ident[:, 0:1])
         nc.vector.tensor_tensor(
@@ -90,47 +99,15 @@ def tile_rwkv_timemix_pa_t_kernel(
             scalar2=None,
             op0=ALU.mult,
         )
-        half = const.tile([P, 1], F32)
-        nc.vector.memset(half[:], 0.5)
         it_f = const.tile([P, T], F32)
         nc.vector.tensor_copy(out=it_f[:], in_=it_i[:])
 
-        pt = psum.tile([P, J, P], BF16, name="pt", tag="aux", bufs=3)
-        for j in range(J):
-            nc.tensor.transpose(out=pt[:, j, :], in_=prm[:, j * P : (j + 1) * P], identity=ident[:])
-        pf = const.tile([P, J, 32], F32)
-        nc.vector.tensor_copy(out=pf[:], in_=pt[:, :, 0:32])
-        xpT = const.tile([P, J, B], BF16)
-        nc.vector.tensor_copy(out=xpT[:], in_=pt[:, :, 24:32])
-        negw = const.tile([P, J], F32)
-        nc.vector.tensor_scalar(out=negw[:], in0=pf[:, :, 0], scalar1=-1.0, scalar2=None, op0=ALU.mult)
-        lnb = const.tile([P, J, B], F32)
-        nc.scalar.activation(out=lnb[:], in_=pf[:, :, 16:24], func=AF.Ln)
-        rb0 = const.tile([P, J, B], F32)
-        nc.vector.reciprocal(out=rb0[:], in_=pf[:, :, 16:24])
-        g0 = const.tile([P, J, B], F32)
-        nc.vector.tensor_tensor(out=g0[:], in0=pf[:, :, 8:16], in1=rb0[:], op=ALU.mult)
-        et = const.tile([P, J, B], F32)
-        nc.vector.tensor_scalar(out=et[:], in0=rb0[:], scalar1=EPS, scalar2=None, op0=ALU.mult)
-        g0e = const.tile([P, J, B], F32)
-        nc.vector.tensor_tensor(out=g0e[:], in0=g0[:], in1=et[:], op=ALU.mult)
-        g0h = const.tile([P, J, B], F32)
-        nc.vector.tensor_scalar(out=g0h[:], in0=g0[:], scalar1=0.5, scalar2=None, op0=ALU.mult)
-        beta = const.tile([P, J, B], F32)
-        nc.vector.tensor_tensor(
-            out=beta[:], in0=pf[:, :, 1:2].to_broadcast([P, J, B]), in1=lnb[:], op=ALU.subtract
-        )
-        dtab = const.tile([P, J, T], F32)
-        for j in range(J):
-            nc.scalar.activation(
-                out=dtab[:, j, :], in_=it_f[:], func=AF.Exp, scale=negw[:, j : j + 1]
-            )
-
         xT = {}
         dd = {}
+        xtp = {}
 
         def make_dd(b, j):
-            t = psum.tile([P, T], F32, name="dd", tag="dd", bufs=2)
+            t = bank([P, T], F32, "dd")
             dd[(b, j)] = t
             for i in range(4):
                 nc.tensor.matmul(
@@ -142,25 +119,24 @@ def tile_rwkv_timemix_pa_t_kernel(
                 )
             nc.tensor.matmul(
                 out=t[:].rearrange("p (i e) -> p i e", e=P)[:, :, 0:8],
-                lhsT=prm[:, j * P : (j + 1) * P],
+                lhsT=prma[:, j * P : (j + 1) * P],
                 rhs=sel[:, b, :, :],
                 start=False,
                 stop=True,
             )
 
-        xtp = {}
-
-        def transposes(b, jh):
-            xt = psum.tile([P, 2, T], BF16, name="xt", tag="aux", bufs=3)
-            xtp[(b, jh)] = xt
-            for jj in range(2):
-                j = 2 * jh + jj
-                for i in range(4):
-                    nc.tensor.transpose(
-                        out=xt[:, jj, i * P : (i + 1) * P],
-                        in_=xn[b][:, i, j * P : (j + 1) * P],
-                        identity=ident[:],
-                    )
+        def transposes(b):
+            for jh in range(2):
+                xt = bank([P, 2, T], BF16, "xt")
+                xtp[(b, jh)] = xt
+                for jj in range(2):
+                    j = 2 * jh + jj
+                    for i in range(4):
+                        nc.tensor.transpose(
+                            out=xt[:, jj, i * P : (i + 1) * P],
+                            in_=xn[b][:, i, j * P : (j + 1) * P],
+                            identity=ident[:],
+                        )
 
         def evac_xT(b):
             xT[b] = work.tile([P, J, PADC + T], BF16, name="xT", tag="xT", bufs=2)
@@ -173,9 +149,9 @@ def tile_rwkv_timemix_pa_t_kernel(
         wg = {}
 
         def prep_w(key):
-            wg[key] = const.tile([P, C, J], BF16, name="wg", tag="wg", bufs=2, align_bytes=64)
+            wg[key] = const.tile([P, C, J], BF16, name="wg", tag="wg", bufs=3, align_bytes=64)
             for h in range(2):
-                wt = psum.tile([P, 2, J, P], BF16, name="wt", tag="aux", bufs=3)
+                wt = bank([P, 2, J, P], BF16, "wt")
                 for a in range(2):
                     for j in range(J):
                         nc.tensor.transpose(
@@ -210,7 +186,7 @@ def tile_rwkv_timemix_pa_t_kernel(
             nc.vector.scalar_tensor_tensor(
                 out=pl[m][:, j, :],
                 in0=dd[(b, j)][:],
-                scalar=pf[:, j, 2 + mi : 3 + mi],
+                scalar=pfa[:, j, mi : mi + 1],
                 in1=xT[b][:, j, PADC - 1 : PADC - 1 + T],
                 op0=ALU.mult,
                 op1=ALU.add,
@@ -218,16 +194,10 @@ def tile_rwkv_timemix_pa_t_kernel(
 
         def regroup(b, m):
             gr[m] = work.tile([P, T, J], BF16, name="gr", tag="gr", bufs=3, align_bytes=64)
-            dst = gr[m][:].rearrange("p (c i) t -> p c t i", i=4)
-            src = pl[m][:].rearrange("p t (c i) -> p c t i", i=4)
-            if G_ENG[m] == "dve":
-                nc.vector.tensor_copy(out=dst, in_=src)
-            elif G_ENG[m] == "act":
-                nc.scalar.copy(out=dst, in_=src)
-            else:
-                nc.gpsimd.tensor_scalar(
-                    out=dst, in0=src, scalar1=1.0, scalar2=0.0, op0=ALU.mult, op1=ALU.add
-                )
+            nc.vector.tensor_copy(
+                out=gr[m][:].rearrange("p (c i) t -> p c t i", i=4),
+                in_=pl[m][:].rearrange("p t (c i) -> p c t i", i=4),
+            )
 
         def quant_x(b, m):
             xc[(b, m)] = work.tile([P, T], U32, name="xc" + m, tag="xc" + m, bufs=2, align_bytes=64)
@@ -242,57 +212,59 @@ def tile_rwkv_timemix_pa_t_kernel(
         th = {}
         qq = {}
         dn = {}
+        ps = {}
 
-        def stage1(b, j):
-            if j == 0:
-                ee[b] = work.tile([P, J, T], F32, name="ee", tag="ee", bufs=2)
-                th[b] = work.tile([P, J, T], F32, name="th", tag="th", bufs=2)
-                qq[b] = work.tile([P, J, T], F32, name="qq", tag="qq", bufs=2)
-                dn[b] = work.tile([P, J, T], F32, name="dn", tag="dn", bufs=2)
-            ps = {}
-            for m in ("k", "r", "v"):
-                ps[m] = psum.tile([P, T], F32, name="s1" + m, tag="s1", bufs=3)
-                nc.tensor.matmul_mx(
-                    out=ps[m][:],
-                    lhsT=wc[m][:, j * P : (j + 1) * P].bitcast(FP8X4),
-                    lhsT_scale=ws[m][:, j * P : (j + 1) * P],
-                    rhs=xc[(b, m)][:].bitcast(FP8X4),
-                    rhs_scale=xs[(b, m)][:],
-                    start=True,
-                    stop=True,
-                )
+        def alloc_b(b):
+            ee[b] = work.tile([P, J, T], F32, name="ee", tag="ee", bufs=2)
+            th[b] = work.tile([P, J, T], F32, name="th", tag="th", bufs=2)
+            qq[b] = work.tile([P, J, T], F32, name="qq", tag="qq", bufs=2)
+            dn[b] = work.tile([P, J, T], F32, name="dn", tag="dn", bufs=2)
+
+        def s1_mm(b, j, m):
+            ps[(b, j, m)] = bank([P, T], F32, "s1" + m)
+            nc.tensor.matmul_mx(
+                out=ps[(b, j, m)][:],
+                lhsT=wc[m][:, j * P : (j + 1) * P].bitcast(FP8X4),
+                lhsT_scale=ws[m][:, j * P : (j + 1) * P],
+                rhs=xc[(b, m)][:].bitcast(FP8X4),
+                rhs_scale=xs[(b, m)][:],
+                start=True,
+                stop=True,
+            )
+
+        def e_exp(b, j):
             nc.scalar.activation(
-                out=ee[b][:, j, :], in_=ps["k"][:], func=AF.Exp, bias=beta[:, j, b : b + 1]
+                out=ee[b][:, j, :], in_=ps[(b, j, "k")][:], func=AF.Exp, bias=beta[:, j, b : b + 1]
             )
-            nc.scalar.activation(out=th[b][:, j, :], in_=ps["r"][:], func=AF.Tanh, scale=0.5)
-            nc.gpsimd.tensor_scalar(
-                out=th[b][:, j, :],
-                in0=th[b][:, j, :],
-                scalar1=1.0,
-                scalar2=1.0,
-                op0=ALU.mult,
-                op1=ALU.add,
-            )
-            nc.gpsimd.tensor_tensor(
-                out=dn[b][:, j, :], in0=ee[b][:, j, :], in1=dtab[:, j, :], op=ALU.add
-            )
+
+        def e_tanh(b, j):
+            nc.scalar.activation(out=th[b][:, j, :], in_=ps[(b, j, "r")][:], func=AF.Tanh, scale=0.5)
+
+        def den(b, j, eng):
+            eng.tensor_tensor(out=dn[b][:, j, :], in0=ee[b][:, j, :], in1=dtab[:, j, :], op=ALU.add)
+
+        def d_q(b, j):
             nc.vector.scalar_tensor_tensor(
                 out=qq[b][:, j, :],
-                in0=ps["v"][:],
+                in0=ps[(b, j, "v")][:],
                 scalar=g0[:, j, b : b + 1],
                 in1=ee[b][:, j, :],
                 op0=ALU.subtract,
                 op1=ALU.mult,
             )
 
-        def recip(b):
-            for j in range(J):
-                nc.scalar.activation(
-                    out=dn[b][:, j, :], in_=dn[b][:, j, :], func=AF.Ln, bias=et[:, j, b : b + 1]
-                )
+        def a_ln(b, j):
+            nc.scalar.activation(
+                out=dn[b][:, j, :], in_=dn[b][:, j, :], func=AF.Ln, bias=et[:, j, b : b + 1]
+            )
+
+        def a_rho(b):
             nc.scalar.activation(out=dn[b][:], in_=dn[b][:], func=AF.Exp, scale=-1.0)
 
-        def wkv_x(b, j):
+        def a_rhoj(b, j):
+            nc.scalar.activation(out=dn[b][:, j, :], in_=dn[b][:, j, :], func=AF.Exp, scale=-1.0)
+
+        def d_x(b, j):
             nc.vector.scalar_tensor_tensor(
                 out=qq[b][:, j, :],
                 in0=qq[b][:, j, :],
@@ -302,136 +274,251 @@ def tile_rwkv_timemix_pa_t_kernel(
                 op1=ALU.mult,
             )
 
-        def wkv_y(b, j):
-            if Y_ENG == "act":
-                nc.scalar.activation(
-                    out=qq[b][:, j, :],
-                    in_=qq[b][:, j, :],
-                    func=AF.Identity,
-                    scale=0.5,
-                    bias=g0h[:, j, b : b + 1],
-                )
-            else:
-                eng = nc.gpsimd if Y_ENG == "pool" else nc.vector
-                eng.tensor_scalar(
-                    out=qq[b][:, j, :],
-                    in0=qq[b][:, j, :],
-                    scalar1=half[:, 0:1],
-                    scalar2=g0h[:, j, b : b + 1],
-                    op0=ALU.mult,
-                    op1=ALU.add,
-                )
+        def y_act(b, j):
+            nc.scalar.activation(
+                out=qq[b][:, j, :],
+                in_=qq[b][:, j, :],
+                func=AF.Identity,
+                scale=0.5,
+                bias=g0h[:, j, b : b + 1],
+            )
+
+        def y_dve(b, j):
+            nc.vector.tensor_scalar(
+                out=qq[b][:, j, :],
+                in0=qq[b][:, j, :],
+                scalar1=half[:, 0:1],
+                scalar2=g0h[:, j, b : b + 1],
+                op0=ALU.mult,
+                op1=ALU.add,
+            )
 
         hg = {}
         hc = {}
         hs = {}
 
-        def gate(b):
-            hg[b] = work.tile([P, T, J], BF16, name="hg", tag="hg", bufs=2, align_bytes=64)
-            nc.vector.tensor_tensor(
-                out=hg[b][:].rearrange("p (c i) j -> p c j i", i=4),
-                in0=th[b][:].rearrange("p j (c i) -> p c j i", i=4),
-                in1=qq[b][:].rearrange("p j (c i) -> p c j i", i=4),
-                op=ALU.mult,
+        def gate(b, h, nh):
+            if h == 0:
+                hg[b] = work.tile([P, T, J], BF16, name="hg", tag="hg", bufs=2, align_bytes=64)
+            n = T // nh
+            nc.vector.scalar_tensor_tensor(
+                out=hg[b][:, h * n : (h + 1) * n, :],
+                in0=th[b][:, :, h * n : (h + 1) * n].rearrange("p j t -> p t j"),
+                scalar=1.0,
+                in1=qq[b][:, :, h * n : (h + 1) * n].rearrange("p j t -> p t j"),
+                op0=ALU.add,
+                op1=ALU.mult,
             )
 
-        def quant_h(b):
-            hc[b] = work.tile([P, T], U32, name="hc", tag="hc", bufs=2, align_bytes=64)
-            hs[b] = work.tile([P, T], U8, name="hs", tag="hs", bufs=2, align_bytes=64)
+        def quant_h(b, h, nh):
+            if h == 0:
+                hc[b] = work.tile([P, T], U32, name="hc", tag="hc", bufs=2, align_bytes=64)
+                hs[b] = work.tile([P, T], U8, name="hs", tag="hs", bufs=2, align_bytes=64)
+            n = T // nh
             nc.vector.quantize_mx(
-                out=hc[b][:].bitcast(FP8X4),
-                scales=hs[b][:],
-                in_=hg[b][:].rearrange("p w t -> p (w t)"),
+                out=hc[b][:, h * n : (h + 1) * n].bitcast(FP8X4),
+                scales=hs[b][:, h * n : (h + 1) * n],
+                in_=hg[b][:, h * n : (h + 1) * n, :].rearrange("p w t -> p (w t)"),
             )
 
-        def stage2(b):
-            ost = work.tile([P, 4, C], F32, name="ost", tag="ost", bufs=2)
-            for i in range(4):
-                po = psum.tile([P, C], F32, name="po", tag="aux", bufs=3)
-                nc.tensor.matmul_mx(
-                    out=po[:],
-                    lhsT=hc[b][:, i * P : (i + 1) * P].bitcast(FP8X4),
-                    lhsT_scale=hs[b][:, i * P : (i + 1) * P],
-                    rhs=wc["o"][:].bitcast(FP8X4),
-                    rhs_scale=ws["o"][:],
-                    start=True,
-                    stop=True,
-                )
-                nc.scalar.copy(out=ost[:, i, :], in_=po[:])
-            nc.sync.dma_start(out=out[b].rearrange("(i p) c -> p i c", p=P), in_=ost[:])
+        po = {}
+        ost = {}
 
-        transposes(0, 0)
-        transposes(0, 1)
+        def s2_mm(b, i):
+            po[(b, i)] = bank([P, C], F32, "po")
+            nc.tensor.matmul_mx(
+                out=po[(b, i)][:],
+                lhsT=hc[b][:, i * P : (i + 1) * P].bitcast(FP8X4),
+                lhsT_scale=hs[b][:, i * P : (i + 1) * P],
+                rhs=wc["o"][:].bitcast(FP8X4),
+                rhs_scale=ws["o"][:],
+                start=True,
+                stop=True,
+            )
+
+        def ao(b, i, on_vector):
+            if i == 0:
+                ost[b] = work.tile([P, 4, C], F32, name="ost", tag="ost", bufs=2)
+            if on_vector:
+                nc.vector.tensor_copy(out=ost[b][:, i, :], in_=po[(b, i)][:])
+            else:
+                nc.scalar.copy(out=ost[b][:, i, :], in_=po[(b, i)][:])
+
+        def store(b, h, nh):
+            n = 4 // nh
+            nc.sync.dma_start(
+                out=out[b, h * n * P : (h + 1) * n * P, :].rearrange("(i p) c -> p i c", p=P),
+                in_=ost[b][:, h * n : (h + 1) * n, :],
+            )
+
+        pta = bank([P, J, P], BF16, "pta")
+        for j in range(J):
+            nc.tensor.transpose(out=pta[:, j, :], in_=prma[:, j * P : (j + 1) * P], identity=ident[:])
+        ptb = bank([P, J, P], BF16, "ptb")
+        for j in range(J):
+            nc.tensor.transpose(out=ptb[:, j, :], in_=prmb[:, j * P : (j + 1) * P], identity=ident[:])
+        pfa = const.tile([P, J, 4], F32)
+        nc.vector.tensor_copy(out=pfa[:], in_=pta[:, :, 0:4])
+        xpT = const.tile([P, J, B], BF16)
+        nc.vector.tensor_copy(out=xpT[:], in_=pta[:, :, 24:32])
+        transposes(0)
         evac_xT(0)
         make_dd(0, 0)
         make_dd(0, 1)
-        for key in ("k", "r", "v"):
-            prep_w(key)
-            if key == "r":
-                quant_w("k")
-        for it in range(B + 2):
-            a = it
-            bb = it - 1
-            c = it - 2
-            has_a = a < B
-            has_n = a + 1 < B
-            has_b = 0 <= bb < B
-            has_c = c >= 0
-            stts = [(j, mi) for j in range(J) for mi in (1, 0, 2)] if has_a else []
-            done = [0]
+        pfb = const.tile([P, J, 24], F32)
+        nc.vector.tensor_copy(out=pfb[:], in_=ptb[:, :, 0:24])
+        negw = const.tile([P, J], F32)
+        nc.vector.tensor_scalar(out=negw[:], in0=pfb[:, :, 0], scalar1=-1.0, scalar2=None, op0=ALU.mult)
+        rb0 = const.tile([P, J, B], F32)
+        nc.vector.reciprocal(out=rb0[:], in_=pfb[:, :, 16:24])
+        g0 = const.tile([P, J, B], F32)
+        nc.vector.tensor_tensor(out=g0[:], in0=pfb[:, :, 8:16], in1=rb0[:], op=ALU.mult)
+        et = const.tile([P, J, B], F32)
+        nc.vector.tensor_scalar(out=et[:], in0=rb0[:], scalar1=EPS, scalar2=None, op0=ALU.mult)
+        g0e = const.tile([P, J, B], F32)
+        nc.vector.tensor_tensor(out=g0e[:], in0=g0[:], in1=et[:], op=ALU.mult)
+        g0h = const.tile([P, J, B], F32)
+        nc.vector.tensor_scalar(out=g0h[:], in0=g0[:], scalar1=0.5, scalar2=None, op0=ALU.mult)
+        lnb = const.tile([P, J, B], F32)
+        nc.scalar.activation(out=lnb[:], in_=pfb[:, :, 16:24], func=AF.Ln)
+        dtab = const.tile([P, J, T], F32)
+        for j in range(J):
+            nc.scalar.activation(
+                out=dtab[:, j, :], in_=it_f[:], func=AF.Exp, scale=negw[:, j : j + 1]
+            )
+        beta = const.tile([P, J, B], F32)
 
-            def emit_stt(n):
-                for q in range(n):
-                    if done[0] < len(stts):
-                        j, mi = stts[done[0]]
-                        mix(a, j, mi)
-                        done[0] += 1
-                        if done[0] == 3:
-                            make_dd(a, 2)
-                        if done[0] == 6:
-                            make_dd(a, 3)
-                        if done[0] == 9 and has_n:
-                            make_dd(a + 1, 0)
-                        if done[0] == 12 and has_n:
-                            make_dd(a + 1, 1)
-
-            if a + 2 < B:
-                load_x(a + 2)
-            for j in range(J):
-                if has_b:
-                    stage1(bb, j)
-                if has_n and j < 2:
-                    transposes(a + 1, j)
-                emit_stt(1)
-            if has_n:
-                evac_xT(a + 1)
-            if has_c:
+        for m in range(B):
+            has_n = m + 1 < B
+            h1 = m >= 1
+            h2 = m >= 2
+            h3 = m >= 3
+            if h1 and m + 2 < B:
+                load_x(m + 2)
+            if h1:
+                alloc_b(m - 1)
                 for j in range(J):
-                    wkv_x(c, j)
+                    s1_mm(m - 1, j, "k")
                 for j in range(J):
-                    wkv_y(c, j)
-            emit_stt(3)
-            if it == 1:
+                    e_exp(m - 1, j)
+                    den(m - 1, j, nc.gpsimd)
+                    s1_mm(m - 1, j, "r")
+                for j in range(J):
+                    e_tanh(m - 1, j)
+                    s1_mm(m - 1, j, "v")
+            qd = 0
+            for s in range(13):
+                while h1 and qd < J and QPOS[qd] <= s:
+                    d_q(m - 1, qd)
+                    qd += 1
+                if s < 12:
+                    mix(m, s // 3, (0, 2, 1)[s % 3])
+                    if s == 2:
+                        make_dd(m, 2)
+                    if s == 5:
+                        make_dd(m, 3)
+                    if s == 8 and has_n:
+                        make_dd(m + 1, 0)
+                    if s == 11 and has_n:
+                        make_dd(m + 1, 1)
+                if m == 0 and s == 2:
+                    prep_w("k")
+                    transposes(1)
+                    evac_xT(1)
+                    prep_w("r")
+                if m == 0 and s == 8:
+                    prep_w("v")
+            if h1:
+                for j in range(J):
+                    a_ln(m - 1, j)
+            if h3:
+                for i in range(4):
+                    s2_mm(m - 3, i)
+                    ao(m - 3, i, False)
+                store(m - 3, 0, 1)
+            if m == 1:
                 prep_w("o")
-            if has_c:
-                gate(c)
-            emit_stt(2)
-            if it == 0:
+            if h2:
+                for j in range(J):
+                    d_x(m - 2, j)
+                for j in range(J):
+                    y_act(m - 2, j)
+            if h1:
+                a_rho(m - 1)
+            if h1 and has_n:
+                transposes(m + 1)
+                evac_xT(m + 1)
+            if m == 0:
+                nc.vector.tensor_tensor(
+                    out=beta[:], in0=pfb[:, :, 1:2].to_broadcast([P, J, B]), in1=lnb[:], op=ALU.subtract
+                )
+            regroup(m, "r")
+            regroup(m, "v")
+            regroup(m, "k")
+            if h2:
+                gate(m - 2, 0, 1)
+            if m == 0:
+                quant_w("k")
+            quant_x(m, "k")
+            if m == 0:
                 quant_w("r")
+            quant_x(m, "r")
+            if m == 0:
                 quant_w("v")
-            if it == 1:
+            if m == 1:
                 quant_w("o")
-            if has_c:
-                quant_h(c)
-            emit_stt(3)
-            if has_b:
-                recip(bb)
-            if has_c:
-                stage2(c)
-            if has_a:
-                regroup(a, "k")
-                regroup(a, "r")
-                quant_x(a, "k")
-                regroup(a, "v")
-                quant_x(a, "r")
-                quant_x(a, "v")
+            quant_x(m, "v")
+            if h2:
+                quant_h(m - 2, 0, 1)
+
+        l7 = B - 1
+        l6 = B - 2
+        l5 = B - 3
+        alloc_b(l7)
+        for j in range(J):
+            s1_mm(l7, j, "k")
+        for j in range(J):
+            e_exp(l7, j)
+            den(l7, j, nc.vector)
+        for j in range(J):
+            s1_mm(l7, j, "v")
+        for j in range(J):
+            d_q(l7, j)
+        for j in range(J):
+            a_ln(l7, j)
+        for i in range(4):
+            s2_mm(l5, i)
+            ao(l5, i, True)
+        store(l5, 0, 1)
+        for j in range(J):
+            d_x(l6, j)
+        for j in range(J):
+            y_dve(l6, j)
+        for j in range(J):
+            a_rhoj(l7, j)
+        for j in range(J):
+            s1_mm(l7, j, "r")
+        for j in range(J):
+            e_tanh(l7, j)
+        gate(l6, 0, 1)
+        d_x(l7, 0)
+        d_x(l7, 1)
+        quant_h(l6, 0, 1)
+        d_x(l7, 2)
+        d_x(l7, 3)
+        for j in range(J):
+            y_dve(l7, j)
+        for i in range(4):
+            s2_mm(l6, i)
+            ao(l6, i, False)
+        store(l6, 0, 1)
+        for h in range(NH):
+            gate(l7, h, NH)
+            if h > 0:
+                quant_h(l7, h - 1, NH)
+        quant_h(l7, NH - 1, NH)
+        for h in range(NH):
+            for i in range(h * 4 // NH, (h + 1) * 4 // NH):
+                s2_mm(l7, i)
+                ao(l7, i, i % 2 == 1)
+            store(l7, h, NH)

@@ -21,7 +21,7 @@ EPS = 1e-8
 PADC = 16
 FLOPS = 4 * 2 * B * T * C * C
 MANUAL = True
-QPOS = (4, 6, 8, 10)
+QPOS = (8, 9, 10, 11)
 NH = 2
 
 
@@ -192,12 +192,22 @@ def tile_rwkv_timemix_pa_t_kernel(
                 op1=ALU.add,
             )
 
-        def regroup(b, m):
+        def regroup(b, m, on_pool):
             gr[m] = work.tile([P, T, J], BF16, name="gr", tag="gr", bufs=3, align_bytes=64)
-            nc.vector.tensor_copy(
-                out=gr[m][:].rearrange("p (c i) t -> p c t i", i=4),
-                in_=pl[m][:].rearrange("p t (c i) -> p c t i", i=4),
-            )
+            if on_pool:
+                nc.gpsimd.tensor_scalar(
+                    out=gr[m][:],
+                    in0=pl[m][:].rearrange("p t w -> p w t"),
+                    scalar1=1.0,
+                    scalar2=0.0,
+                    op0=ALU.mult,
+                    op1=ALU.add,
+                )
+            else:
+                nc.vector.tensor_copy(
+                    out=gr[m][:].rearrange("p (c i) t -> p c t i", i=4),
+                    in_=pl[m][:].rearrange("p t (c i) -> p c t i", i=4),
+                )
 
         def quant_x(b, m):
             xc[(b, m)] = work.tile([P, T], U32, name="xc" + m, tag="xc" + m, bufs=2, align_bytes=64)
@@ -363,8 +373,8 @@ def tile_rwkv_timemix_pa_t_kernel(
         nc.vector.tensor_copy(out=xpT[:], in_=pta[:, :, 24:32])
         transposes(0)
         evac_xT(0)
-        make_dd(0, 0)
-        make_dd(0, 1)
+        for j in range(J):
+            make_dd(0, j)
         pfb = const.tile([P, J, 24], F32)
         nc.vector.tensor_copy(out=pfb[:], in_=ptb[:, :, 0:24])
         negw = const.tile([P, J], F32)
@@ -412,15 +422,11 @@ def tile_rwkv_timemix_pa_t_kernel(
                     d_q(m - 1, qd)
                     qd += 1
                 if s < 12:
-                    mix(m, s // 3, (0, 2, 1)[s % 3])
-                    if s == 2:
-                        make_dd(m, 2)
-                    if s == 5:
-                        make_dd(m, 3)
-                    if s == 8 and has_n:
-                        make_dd(m + 1, 0)
-                    if s == 11 and has_n:
-                        make_dd(m + 1, 1)
+                    mix(m, s % 4, (1, 0, 2)[s // 4])
+                    if s >= 8 and has_n:
+                        make_dd(m + 1, s % 4)
+                    if s == 3:
+                        regroup(m, "k", True)
                 if m == 0 and s == 2:
                     prep_w("k")
                     transposes(1)
@@ -452,14 +458,13 @@ def tile_rwkv_timemix_pa_t_kernel(
                 nc.vector.tensor_tensor(
                     out=beta[:], in0=pfb[:, :, 1:2].to_broadcast([P, J, B]), in1=lnb[:], op=ALU.subtract
                 )
-            regroup(m, "r")
-            regroup(m, "v")
-            regroup(m, "k")
-            if h2:
-                gate(m - 2, 0, 1)
+            regroup(m, "r", False)
+            regroup(m, "v", False)
             if m == 0:
                 quant_w("k")
             quant_x(m, "k")
+            if h2:
+                gate(m - 2, 0, 1)
             if m == 0:
                 quant_w("r")
             quant_x(m, "r")

@@ -21,7 +21,7 @@ EPS = 1e-8
 PADC = 16
 FLOPS = 4 * 2 * B * T * C * C
 MANUAL = True
-QPOS = (8, 9, 10, 11)
+QPOS = (10, 11, 12, 12)
 NH = 2
 
 
@@ -427,6 +427,8 @@ def tile_rwkv_timemix_pa_t_kernel(
                         make_dd(m + 1, s % 4)
                     if s == 3:
                         regroup(m, "k", True)
+                    if s == 7 and m == 0:
+                        regroup(m, "r", True)
                 if m == 0 and s == 2:
                     prep_w("k")
                     transposes(1)
@@ -449,16 +451,17 @@ def tile_rwkv_timemix_pa_t_kernel(
                     d_x(m - 2, j)
                 for j in range(J):
                     y_act(m - 2, j)
-            if h1:
-                a_rho(m - 1)
             if h1 and has_n:
                 transposes(m + 1)
                 evac_xT(m + 1)
+            if h1:
+                a_rho(m - 1)
             if m == 0:
                 nc.vector.tensor_tensor(
                     out=beta[:], in0=pfb[:, :, 1:2].to_broadcast([P, J, B]), in1=lnb[:], op=ALU.subtract
                 )
-            regroup(m, "r", False)
+            if m > 0:
+                regroup(m, "r", False)
             regroup(m, "v", False)
             if m == 0:
                 quant_w("k")
@@ -491,10 +494,6 @@ def tile_rwkv_timemix_pa_t_kernel(
             d_q(l7, j)
         for j in range(J):
             a_ln(l7, j)
-        for i in range(4):
-            s2_mm(l5, i)
-            ao(l5, i, True)
-        store(l5, 0, 1)
         for j in range(J):
             d_x(l6, j)
         for j in range(J):
@@ -505,6 +504,10 @@ def tile_rwkv_timemix_pa_t_kernel(
             s1_mm(l7, j, "r")
         for j in range(J):
             e_tanh(l7, j)
+        for i in range(4):
+            s2_mm(l5, i)
+            ao(l5, i, False)
+        store(l5, 0, 1)
         gate(l6, 0, 1)
         d_x(l7, 0)
         d_x(l7, 1)

@@ -22,7 +22,7 @@ PADC = 16
 FLOPS = 4 * 2 * B * T * C * C
 MANUAL = True
 QPOS = (10, 11, 12, 12)
-NH = 2
+NH = 4
 
 
 def tile_rwkv_timemix_pa_t_kernel(
@@ -56,23 +56,22 @@ def tile_rwkv_timemix_pa_t_kernel(
 
         xn = {}
 
-        def load_x(b):
+        def load_x(b, queue):
             xn[b] = work.tile([P, 4, C], BF16, name="xn", tag="xn", bufs=3)
-            nc.sync.dma_start(out=xn[b][:], in_=x[b].rearrange("(i p) c -> p i c", p=P))
+            queue.dma_start(out=xn[b][:], in_=x[b].rearrange("(i p) c -> p i c", p=P))
 
         wnat = {}
 
         def load_w(key, wap):
             wnat[key] = const.tile([P, 4, C], BF16, name="wn" + key, tag="wn" + key)
-            nc.sync.dma_start(out=wnat[key][:], in_=wap.rearrange("(a p) c -> p a c", p=P))
+            nc.scalar.dma_start(out=wnat[key][:], in_=wap.rearrange("(a p) c -> p a c", p=P))
 
-        load_x(0)
-        load_w("k", W_k)
-        load_w("r", W_r)
-        load_w("v", W_v)
-        load_x(1)
-        load_w("o", W_out)
-        load_x(2)
+        xn[0] = work.tile([P, 4, C], BF16, name="xn", tag="xn", bufs=3)
+        for hh in range(2):
+            nc.sync.dma_start(
+                out=xn[0][:, :, hh * 256 : (hh + 1) * 256],
+                in_=x[0, :, hh * 256 : (hh + 1) * 256].rearrange("(i p) c -> p i c", p=P),
+            )
 
         ident = const.tile([P, P], BF16)
         masks.make_identity(nc, ident[:])
@@ -82,6 +81,12 @@ def tile_rwkv_timemix_pa_t_kernel(
         nc.vector.memset(half[:], 0.5)
         dummy = const.tile([P, 1], F32)
         nc.scalar.activation(out=dummy[:], in_=half[:], func=AF.Ln)
+        load_w("k", W_k)
+        load_w("r", W_r)
+        load_w("v", W_v)
+        load_x(1, nc.scalar)
+        load_w("o", W_out)
+        load_x(2, nc.scalar)
         dmat = const.tile([P, P], BF16)
         nc.vector.tensor_copy(out=dmat[:, 0:1], in_=ident[:, 0:1])
         nc.vector.tensor_tensor(
@@ -125,8 +130,8 @@ def tile_rwkv_timemix_pa_t_kernel(
                 stop=True,
             )
 
-        def transposes(b):
-            for jh in range(2):
+        def transposes(b, halves):
+            for jh in halves:
                 xt = bank([P, 2, T], BF16, "xt")
                 xtp[(b, jh)] = xt
                 for jj in range(2):
@@ -364,17 +369,20 @@ def tile_rwkv_timemix_pa_t_kernel(
         pta = bank([P, J, P], BF16, "pta")
         for j in range(J):
             nc.tensor.transpose(out=pta[:, j, :], in_=prma[:, j * P : (j + 1) * P], identity=ident[:])
-        ptb = bank([P, J, P], BF16, "ptb")
-        for j in range(J):
-            nc.tensor.transpose(out=ptb[:, j, :], in_=prmb[:, j * P : (j + 1) * P], identity=ident[:])
         pfa = const.tile([P, J, 4], F32)
         nc.vector.tensor_copy(out=pfa[:], in_=pta[:, :, 0:4])
         xpT = const.tile([P, J, B], BF16)
         nc.vector.tensor_copy(out=xpT[:], in_=pta[:, :, 24:32])
-        transposes(0)
+        transposes(0, (0,))
+        make_dd(0, 0)
+        make_dd(0, 1)
+        transposes(0, (1,))
+        make_dd(0, 2)
+        make_dd(0, 3)
         evac_xT(0)
+        ptb = bank([P, J, P], BF16, "ptb")
         for j in range(J):
-            make_dd(0, j)
+            nc.tensor.transpose(out=ptb[:, j, :], in_=prmb[:, j * P : (j + 1) * P], identity=ident[:])
         pfb = const.tile([P, J, 24], F32)
         nc.vector.tensor_copy(out=pfb[:], in_=ptb[:, :, 0:24])
         negw = const.tile([P, J], F32)
@@ -392,10 +400,6 @@ def tile_rwkv_timemix_pa_t_kernel(
         lnb = const.tile([P, J, B], F32)
         nc.scalar.activation(out=lnb[:], in_=pfb[:, :, 16:24], func=AF.Ln)
         dtab = const.tile([P, J, T], F32)
-        for j in range(J):
-            nc.scalar.activation(
-                out=dtab[:, j, :], in_=it_f[:], func=AF.Exp, scale=negw[:, j : j + 1]
-            )
         beta = const.tile([P, J, B], F32)
 
         for m in range(B):
@@ -404,13 +408,17 @@ def tile_rwkv_timemix_pa_t_kernel(
             h2 = m >= 2
             h3 = m >= 3
             if h1 and m + 2 < B:
-                load_x(m + 2)
+                load_x(m + 2, nc.sync)
             if h1:
                 alloc_b(m - 1)
                 for j in range(J):
                     s1_mm(m - 1, j, "k")
                 for j in range(J):
                     e_exp(m - 1, j)
+                    if m == 1:
+                        nc.scalar.activation(
+                            out=dtab[:, j, :], in_=it_f[:], func=AF.Exp, scale=negw[:, j : j + 1]
+                        )
                     den(m - 1, j, nc.gpsimd)
                     s1_mm(m - 1, j, "r")
                 for j in range(J):
@@ -431,7 +439,7 @@ def tile_rwkv_timemix_pa_t_kernel(
                         regroup(m, "r", True)
                 if m == 0 and s == 2:
                     prep_w("k")
-                    transposes(1)
+                    transposes(1, (0, 1))
                     evac_xT(1)
                     prep_w("r")
                 if m == 0 and s == 8:
@@ -452,7 +460,7 @@ def tile_rwkv_timemix_pa_t_kernel(
                 for j in range(J):
                     y_act(m - 2, j)
             if h1 and has_n:
-                transposes(m + 1)
+                transposes(m + 1, (0, 1))
                 evac_xT(m + 1)
             if h1:
                 a_rho(m - 1)

@@ -23,6 +23,7 @@ FLOPS = 4 * 2 * B * T * C * C
 MANUAL = True
 QPOS = (10, 11, 12, 12)
 NH = 4
+YSPLIT = 3
 
 
 def tile_rwkv_timemix_pa_t_kernel(
@@ -76,7 +77,6 @@ def tile_rwkv_timemix_pa_t_kernel(
         ident = const.tile([P, P], BF16)
         masks.make_identity(nc, ident[:])
         it_i = const.tile([P, T], I32)
-        nc.gpsimd.iota(it_i[:], pattern=[[1, T]], base=1, channel_multiplier=0)
         half = const.tile([P, 1], F32)
         nc.vector.memset(half[:], 0.5)
         dummy = const.tile([P, 1], F32)
@@ -105,7 +105,6 @@ def tile_rwkv_timemix_pa_t_kernel(
             op0=ALU.mult,
         )
         it_f = const.tile([P, T], F32)
-        nc.vector.tensor_copy(out=it_f[:], in_=it_i[:])
 
         xT = {}
         dd = {}
@@ -437,6 +436,7 @@ def tile_rwkv_timemix_pa_t_kernel(
                         regroup(m, "k", True)
                     if s == 7 and m == 0:
                         regroup(m, "r", True)
+                        nc.gpsimd.iota(it_i[:], pattern=[[1, T]], base=1, channel_multiplier=0)
                 if m == 0 and s == 2:
                     prep_w("k")
                     transposes(1, (0, 1))
@@ -458,7 +458,10 @@ def tile_rwkv_timemix_pa_t_kernel(
                 for j in range(J):
                     d_x(m - 2, j)
                 for j in range(J):
-                    y_act(m - 2, j)
+                    if j < YSPLIT:
+                        y_act(m - 2, j)
+                    else:
+                        y_dve(m - 2, j)
             if h1 and has_n:
                 transposes(m + 1, (0, 1))
                 evac_xT(m + 1)
@@ -468,6 +471,7 @@ def tile_rwkv_timemix_pa_t_kernel(
                 nc.vector.tensor_tensor(
                     out=beta[:], in0=pfb[:, :, 1:2].to_broadcast([P, J, B]), in1=lnb[:], op=ALU.subtract
                 )
+                nc.vector.tensor_copy(out=it_f[:], in_=it_i[:])
             if m > 0:
                 regroup(m, "r", False)
             regroup(m, "v", False)

from contextlib import ExitStack

import concourse.masks as masks
import concourse.mybir as mybir

FP8X4 = mybir.dt.float8_e4m3fn_x4
BF16 = mybir.dt.bfloat16
F32 = mybir.dt.float32
I32 = mybir.dt.int32
U32 = mybir.dt.uint32
U8 = mybir.dt.uint8
ALU = mybir.AluOpType
AF = mybir.ActivationFunctionType

P = 128
B = 8
T = 512
C = 512
J = 4
EPS = 1e-8
PADC = 16
FLOPS = 4 * 2 * B * T * C * C
MANUAL = True
QPOS = (10, 11, 12, 12)
NH = 4
YSPLIT = 3


def tile_rwkv_timemix_pa_t_kernel(
    tc, x, a0, b0, x_prev0, w, u, mu_r, mu_k, mu_v, W_r, W_k, W_v, W_out, out
):
    nc = tc.nc
    with ExitStack() as ctx:
        if MANUAL:
            ctx.enter_context(tc.manual_schedule())
        const = ctx.enter_context(tc.tile_pool(name="const", bufs=1))
        work = ctx.enter_context(tc.tile_pool(name="work", bufs=2))
        psum = ctx.enter_context(tc.psum_pool(name="psum", bufs=8))

        def bank(shape, dtype, name):
            return psum.tile(shape, dtype, name=name, tag="ps", bufs=8)

        prma = const.tile([P, C], BF16)
        prmb = const.tile([P, C], BF16)
        nc.vector.memset(prma[:], 0.0)
        nc.vector.memset(prmb[:], 0.0)
        nc.sync.dma_start(
            out=prma[32:64, :], in_=x.rearrange("b (i t) c -> (b i) t c", t=P)[:, P - 1, :]
        )
        for r, vec in enumerate((mu_r, mu_k, mu_v)):
            nc.scalar.dma_start(out=prma[r : r + 1, :], in_=vec.rearrange("(o c) -> o c", o=1))
        nc.scalar.dma_start(out=prma[24:32, :], in_=x_prev0)
        for r, vec in enumerate((w, u)):
            nc.scalar.dma_start(out=prmb[r : r + 1, :], in_=vec.rearrange("(o c) -> o c", o=1))
        nc.scalar.dma_start(out=prmb[8:16, :], in_=a0)
        nc.scalar.dma_start(out=prmb[16:24, :], in_=b0)

        xn = {}

        def load_x(b, queue):
            xn[b] = work.tile([P, 4, C], BF16, name="xn", tag="xn", bufs=3)
            queue.dma_start(out=xn[b][:], in_=x[b].rearrange("(i p) c -> p i c", p=P))

        wnat = {}

        def load_w(key, wap):
            wnat[key] = const.tile([P, 4, C], BF16, name="wn" + key, tag="wn" + key)
            nc.scalar.dma_start(out=wnat[key][:], in_=wap.rearrange("(a p) c -> p a c", p=P))

        xn[0] = work.tile([P, 4, C], BF16, name="xn", tag="xn", bufs=3)
        for hh in range(2):
            nc.sync.dma_start(
                out=xn[0][:, :, hh * 256 : (hh + 1) * 256],
                in_=x[0, :, hh * 256 : (hh + 1) * 256].rearrange("(i p) c -> p i c", p=P),
            )

        ident = const.tile([P, P], BF16)
        masks.make_identity(nc, ident[:])
        it_i = const.tile([P, T], I32)
        half = const.tile([P, 1], F32)
        nc.vector.memset(half[:], 0.5)
        dummy = const.tile([P, 1], F32)
        nc.scalar.activation(out=dummy[:], in_=half[:], func=AF.Ln)
        load_w("k", W_k)
        load_w("r", W_r)
        load_w("v", W_v)
        load_x(1, nc.scalar)
        load_w("o", W_out)
        load_x(2, nc.scalar)
        dmat = const.tile([P, P], BF16)
        nc.vector.tensor_copy(out=dmat[:, 0:1], in_=ident[:, 0:1])
        nc.vector.tensor_tensor(
            out=dmat[:, 1:P], in0=ident[:, 1:P], in1=ident[:, 0 : P - 1], op=ALU.subtract
        )
        sel = const.tile([P, B, 4, 8], BF16)
        nc.vector.memset(sel[:], 0.0)
        nc.vector.tensor_scalar(
            out=sel[:, :, 0, 0], in0=ident[:, 24:32], scalar1=-1.0, scalar2=None, op0=ALU.mult
        )
        nc.vector.tensor_scalar(
            out=sel[:, :, 1:4, 0],
            in0=ident[:, 32:64].rearrange("p (b i) -> p b i", i=4)[:, :, 0:3],
            scalar1=-1.0,
            scalar2=None,
            op0=ALU.mult,
        )
        it_f = const.tile([P, T], F32)

        xT = {}
        dd = {}
        xtp = {}

        def make_dd(b, j):
            t = bank([P, T], F32, "dd")
            dd[(b, j)] = t
            for i in range(4):
                nc.tensor.matmul(
                    out=t[:, i * P : (i + 1) * P],
                    lhsT=xn[b][:, i, j * P : (j + 1) * P],
                    rhs=dmat[:],
                    start=(i == 0),
                    stop=False,
                )
            nc.tensor.matmul(
                out=t[:].rearrange("p (i e) -> p i e", e=P)[:, :, 0:8],
                lhsT=prma[:, j * P : (j + 1) * P],
                rhs=sel[:, b, :, :],
                start=False,
                stop=True,
            )

        def transposes(b, halves):
            for jh in halves:
                xt = bank([P, 2, T], BF16, "xt")
                xtp[(b, jh)] = xt
                for jj in range(2):
                    j = 2 * jh + jj
                    for i in range(4):
                        nc.tensor.transpose(
                            out=xt[:, jj, i * P : (i + 1) * P],
                            in_=xn[b][:, i, j * P : (j + 1) * P],
                            identity=ident[:],
                        )

        def evac_xT(b):
            xT[b] = work.tile([P, J, PADC + T], BF16, name="xT", tag="xT", bufs=2)
            nc.gpsimd.tensor_copy(out=xT[b][:, :, PADC - 1 : PADC], in_=xpT[:, :, b : b + 1])
            for jh in range(2):
                nc.scalar.copy(out=xT[b][:, 2 * jh : 2 * jh + 2, PADC:], in_=xtp[(b, jh)][:])

        wc = {}
        ws = {}
        wg = {}

        def prep_w(key):
            wg[key] = const.tile([P, C, J], BF16, name="wg", tag="wg", bufs=3, align_bytes=64)
            for h in range(2):
                wt = bank([P, 2, J, P], BF16, "wt")
                for a in range(2):
                    for j in range(J):
                        nc.tensor.transpose(
                            out=wt[:, a, j, :],
                            in_=wnat[key][:, 2 * h + a, j * P : (j + 1) * P],
                            identity=ident[:],
                        )
                nc.scalar.copy(
                    out=wg[key][:, 256 * h : 256 * h + 256, :].rearrange("p (a o) j -> p a o j", a=2),
                    in_=wt[:].rearrange("p a j o -> p a o j"),
                )

        def quant_w(key):
            wc[key] = const.tile([P, C], U32, name="wc" + key, tag="wc" + key, align_bytes=64)
            ws[key] = const.tile([P, C], U8, name="ws" + key, tag="ws" + key, align_bytes=64)
            nc.vector.quantize_mx(
                out=wc[key][:].bitcast(FP8X4),
                scales=ws[key][:],
                in_=wg[key][:].rearrange("p o j -> p (o j)"),
            )

        pl = {}
        gr = {}
        xc = {}
        xs = {}
        MS = ("r", "k", "v")

        def mix(b, j, mi):
            m = MS[mi]
            if j == 0:
                pl[m] = work.tile([P, J, T], BF16, name="pl" + m, tag="pl" + m, bufs=1)
            nc.vector.scalar_tensor_tensor(
                out=pl[m][:, j, :],
                in0=dd[(b, j)][:],
                scalar=pfa[:, j, mi : mi + 1],
                in1=xT[b][:, j, PADC - 1 : PADC - 1 + T],
                op0=ALU.mult,
                op1=ALU.add,
            )

        def regroup(b, m, on_pool):
            gr[m] = work.tile([P, T, J], BF16, name="gr", tag="gr", bufs=3, align_bytes=64)
            if on_pool:
                nc.gpsimd.tensor_scalar(
                    out=gr[m][:],
                    in0=pl[m][:].rearrange("p t w -> p w t"),
                    scalar1=1.0,
                    scalar2=0.0,
                    op0=ALU.mult,
                    op1=ALU.add,
                )
            else:
                nc.vector.tensor_copy(
                    out=gr[m][:].rearrange("p (c i) t -> p c t i", i=4),
                    in_=pl[m][:].rearrange("p t (c i) -> p c t i", i=4),
                )

        def quant_x(b, m):
            xc[(b, m)] = work.tile([P, T], U32, name="xc" + m, tag="xc" + m, bufs=2, align_bytes=64)
            xs[(b, m)] = work.tile([P, T], U8, name="xs" + m, tag="xs" + m, bufs=2, align_bytes=64)
            nc.vector.quantize_mx(
                out=xc[(b, m)][:].bitcast(FP8X4),
                scales=xs[(b, m)][:],
                in_=gr[m][:].rearrange("p w t -> p (w t)"),
            )

        ee = {}
        th = {}
        qq = {}
        dn = {}
        ps = {}

        def alloc_b(b):
            ee[b] = work.tile([P, J, T], F32, name="ee", tag="ee", bufs=2)
            th[b] = work.tile([P, J, T], F32, name="th", tag="th", bufs=2)
            qq[b] = work.tile([P, J, T], F32, name="qq", tag="qq", bufs=2)
            dn[b] = work.tile([P, J, T], F32, name="dn", tag="dn", bufs=2)

        def s1_mm(b, j, m):
            ps[(b, j, m)] = bank([P, T], F32, "s1" + m)
            nc.tensor.matmul_mx(
                out=ps[(b, j, m)][:],
                lhsT=wc[m][:, j * P : (j + 1) * P].bitcast(FP8X4),
                lhsT_scale=ws[m][:, j * P : (j + 1) * P],
                rhs=xc[(b, m)][:].bitcast(FP8X4),
                rhs_scale=xs[(b, m)][:],
                start=True,
                stop=True,
            )

        def e_exp(b, j):
            nc.scalar.activation(
                out=ee[b][:, j, :], in_=ps[(b, j, "k")][:], func=AF.Exp, bias=beta[:, j, b : b + 1]
            )

        def e_tanh(b, j):
            nc.scalar.activation(out=th[b][:, j, :], in_=ps[(b, j, "r")][:], func=AF.Tanh, scale=0.5)

        def den(b, j, eng):
            eng.tensor_tensor(out=dn[b][:, j, :], in0=ee[b][:, j, :], in1=dtab[:, j, :], op=ALU.add)

        def d_q(b, j):
            nc.vector.scalar_tensor_tensor(
                out=qq[b][:, j, :],
                in0=ps[(b, j, "v")][:],
                scalar=g0[:, j, b : b + 1],
                in1=ee[b][:, j, :],
                op0=ALU.subtract,
                op1=ALU.mult,
            )

        def a_ln(b, j):
            nc.scalar.activation(
                out=dn[b][:, j, :], in_=dn[b][:, j, :], func=AF.Ln, bias=et[:, j, b : b + 1]
            )

        def a_rho(b):
            nc.scalar.activation(out=dn[b][:], in_=dn[b][:], func=AF.Exp, scale=-1.0)

        def a_rhoj(b, j):
            nc.scalar.activation(out=dn[b][:, j, :], in_=dn[b][:, j, :], func=AF.Exp, scale=-1.0)

        def d_x(b, j):
            nc.vector.scalar_tensor_tensor(
                out=qq[b][:, j, :],
                in0=qq[b][:, j, :],
                scalar=g0e[:, j, b : b + 1],
                in1=dn[b][:, j, :],
                op0=ALU.subtract,
                op1=ALU.mult,
            )

        def y_act(b, j):
            nc.scalar.activation(
                out=qq[b][:, j, :],
                in_=qq[b][:, j, :],
                func=AF.Identity,
                scale=0.5,
                bias=g0h[:, j, b : b + 1],
            )

        def y_dve(b, j):
            nc.vector.tensor_scalar(
                out=qq[b][:, j, :],
                in0=qq[b][:, j, :],
                scalar1=half[:, 0:1],
                scalar2=g0h[:, j, b : b + 1],
                op0=ALU.mult,
                op1=ALU.add,
            )

        hg = {}
        hc = {}
        hs = {}

        def gate(b, h, nh):
            if h == 0:
                hg[b] = work.tile([P, T, J], BF16, name="hg", tag="hg", bufs=2, align_bytes=64)
            n = T // nh
            nc.vector.scalar_tensor_tensor(
                out=hg[b][:, h * n : (h + 1) * n, :],
                in0=th[b][:, :, h * n : (h + 1) * n].rearrange("p j t -> p t j"),
                scalar=1.0,
                in1=qq[b][:, :, h * n : (h + 1) * n].rearrange("p j t -> p t j"),
                op0=ALU.add,
                op1=ALU.mult,
            )

        def quant_h(b, h, nh):
            if h == 0:
                hc[b] = work.tile([P, T], U32, name="hc", tag="hc", bufs=2, align_bytes=64)
                hs[b] = work.tile([P, T], U8, name="hs", tag="hs", bufs=2, align_bytes=64)
            n = T // nh
            nc.vector.quantize_mx(
                out=hc[b][:, h * n : (h + 1) * n].bitcast(FP8X4),
                scales=hs[b][:, h * n : (h + 1) * n],
                in_=hg[b][:, h * n : (h + 1) * n, :].rearrange("p w t -> p (w t)"),
            )

        po = {}
        ost = {}

        def s2_mm(b, i):
            po[(b, i)] = bank([P, C], F32, "po")
            nc.tensor.matmul_mx(
                out=po[(b, i)][:],
                lhsT=hc[b][:, i * P : (i + 1) * P].bitcast(FP8X4),
                lhsT_scale=hs[b][:, i * P : (i + 1) * P],
                rhs=wc["o"][:].bitcast(FP8X4),
                rhs_scale=ws["o"][:],
                start=True,
                stop=True,
            )

        def ao(b, i, on_vector):
            if i == 0:
                ost[b] = work.tile([P, 4, C], F32, name="ost", tag="ost", bufs=2)
            if on_vector:
                nc.vector.tensor_copy(out=ost[b][:, i, :], in_=po[(b, i)][:])
            else:
                nc.scalar.copy(out=ost[b][:, i, :], in_=po[(b, i)][:])

        def store(b, h, nh):
            n = 4 // nh
            nc.sync.dma_start(
                out=out[b, h * n * P : (h + 1) * n * P, :].rearrange("(i p) c -> p i c", p=P),
                in_=ost[b][:, h * n : (h + 1) * n, :],
            )

        pta = bank([P, J, P], BF16, "pta")
        for j in range(J):
            nc.tensor.transpose(out=pta[:, j, :], in_=prma[:, j * P : (j + 1) * P], identity=ident[:])
        pfa = const.tile([P, J, 4], F32)
        nc.vector.tensor_copy(out=pfa[:], in_=pta[:, :, 0:4])
        xpT = const.tile([P, J, B], BF16)
        nc.vector.tensor_copy(out=xpT[:], in_=pta[:, :, 24:32])
        transposes(0, (0,))
        make_dd(0, 0)
        make_dd(0, 1)
        transposes(0, (1,))
        make_dd(0, 2)
        make_dd(0, 3)
        evac_xT(0)
        ptb = bank([P, J, P], BF16, "ptb")
        for j in range(J):
            nc.tensor.transpose(out=ptb[:, j, :], in_=prmb[:, j * P : (j + 1) * P], identity=ident[:])
        pfb = const.tile([P, J, 24], F32)
        nc.vector.tensor_copy(out=pfb[:], in_=ptb[:, :, 0:24])
        negw = const.tile([P, J], F32)
        nc.vector.tensor_scalar(out=negw[:], in0=pfb[:, :, 0], scalar1=-1.0, scalar2=None, op0=ALU.mult)
        rb0 = const.tile([P, J, B], F32)
        nc.vector.reciprocal(out=rb0[:], in_=pfb[:, :, 16:24])
        g0 = const.tile([P, J, B], F32)
        nc.vector.tensor_tensor(out=g0[:], in0=pfb[:, :, 8:16], in1=rb0[:], op=ALU.mult)
        et = const.tile([P, J, B], F32)
        nc.vector.tensor_scalar(out=et[:], in0=rb0[:], scalar1=EPS, scalar2=None, op0=ALU.mult)
        g0e = const.tile([P, J, B], F32)
        nc.vector.tensor_tensor(out=g0e[:], in0=g0[:], in1=et[:], op=ALU.mult)
        g0h = const.tile([P, J, B], F32)
        nc.vector.tensor_scalar(out=g0h[:], in0=g0[:], scalar1=0.5, scalar2=None, op0=ALU.mult)
        lnb = const.tile([P, J, B], F32)
        nc.scalar.activation(out=lnb[:], in_=pfb[:, :, 16:24], func=AF.Ln)
        dtab = const.tile([P, J, T], F32)
        beta = const.tile([P, J, B], F32)

        for m in range(B):
            has_n = m + 1 < B
            h1 = m >= 1
            h2 = m >= 2
            h3 = m >= 3
            if h1 and m + 2 < B:
                load_x(m + 2, nc.sync)
            if h1:
                alloc_b(m - 1)
                for j in range(J):
                    s1_mm(m - 1, j, "k")
                for j in range(J):
                    e_exp(m - 1, j)
                    if m == 1:
                        nc.scalar.activation(
                            out=dtab[:, j, :], in_=it_f[:], func=AF.Exp, scale=negw[:, j : j + 1]
                        )
                    den(m - 1, j, nc.gpsimd)
                    s1_mm(m - 1, j, "r")
                for j in range(J):
                    e_tanh(m - 1, j)
                    s1_mm(m - 1, j, "v")
            qd = 0
            for s in range(13):
                while h1 and qd < J and QPOS[qd] <= s:
                    d_q(m - 1, qd)
                    qd += 1
                if s < 12:
                    mix(m, s % 4, (1, 0, 2)[s // 4])
                    if s >= 8 and has_n:
                        make_dd(m + 1, s % 4)
                    if s == 3:
                        regroup(m, "k", True)
                    if s == 7 and m == 0:
                        regroup(m, "r", True)
                        nc.gpsimd.iota(it_i[:], pattern=[[1, T]], base=1, channel_multiplier=0)
                if m == 0 and s == 2:
                    prep_w("k")
                    transposes(1, (0, 1))
                    evac_xT(1)
                    prep_w("r")
                if m == 0 and s == 8:
                    prep_w("v")
            if h1:
                for j in range(J):
                    a_ln(m - 1, j)
            if h3:
                for i in range(4):
                    s2_mm(m - 3, i)
                    ao(m - 3, i, False)
                store(m - 3, 0, 1)
            if m == 1:
                prep_w("o")
            if h2:
                for j in range(J):
                    d_x(m - 2, j)
                for j in range(J):
                    if j < YSPLIT:
                        y_act(m - 2, j)
                    else:
                        y_dve(m - 2, j)
            if h1 and has_n:
                transposes(m + 1, (0, 1))
                evac_xT(m + 1)
            if h1:
                a_rho(m - 1)
            if m == 0:
                nc.vector.tensor_tensor(
                    out=beta[:], in0=pfb[:, :, 1:2].to_broadcast([P, J, B]), in1=lnb[:], op=ALU.subtract
                )
                nc.vector.tensor_copy(out=it_f[:], in_=it_i[:])
            if m > 0:
                regroup(m, "r", False)
            regroup(m, "v", False)
            if m == 0:
                quant_w("k")
            quant_x(m, "k")
            if h2:
                gate(m - 2, 0, 1)
            if m == 0:
                quant_w("r")
            quant_x(m, "r")
            if m == 0:
                quant_w("v")
            if m == 1:
                quant_w("o")
            quant_x(m, "v")
            if h2:
                quant_h(m - 2, 0, 1)

        l7 = B - 1
        l6 = B - 2
        l5 = B - 3
        alloc_b(l7)
        for j in range(J):
            s1_mm(l7, j, "k")
        for j in range(J):
            e_exp(l7, j)
            den(l7, j, nc.vector)
        for j in range(J):
            s1_mm(l7, j, "v")
        for j in range(J):
            d_q(l7, j)
        for j in range(J):
            a_ln(l7, j)
        for j in range(J):
            d_x(l6, j)
        for j in range(J):
            y_dve(l6, j)
        for j in range(J):
            a_rhoj(l7, j)
        for j in range(J):
            s1_mm(l7, j, "r")
        for j in range(J):
            e_tanh(l7, j)
        for i in range(4):
            s2_mm(l5, i)
            ao(l5, i, False)
        store(l5, 0, 1)
        gate(l6, 0, 1)
        d_x(l7, 0)
        d_x(l7, 1)
        quant_h(l6, 0, 1)
        d_x(l7, 2)
        d_x(l7, 3)
        for j in range(J):
            y_dve(l7, j)
        for i in range(4):
            s2_mm(l6, i)
            ao(l6, i, False)
        store(l6, 0, 1)
        for h in range(NH):
            gate(l7, h, NH)
            if h > 0:
                quant_h(l7, h - 1, NH)
        quant_h(l7, NH - 1, NH)
        for h in range(NH):
            for i in range(h * 4 // NH, (h + 1) * 4 // NH):
                s2_mm(l7, i)
                ao(l7, i, i % 2 == 1)
            store(l7, h, NH)
